import numpy as np
import ml_dtypes


def mxq(x, axis, fmt="e4m3"):
    dtype, down = {"e4m3": (ml_dtypes.float8_e4m3fn, 7), "e5m2": (ml_dtypes.float8_e5m2, 14)}[fmt]
    v = np.moveaxis(np.asarray(x, np.float32).astype(ml_dtypes.bfloat16).astype(np.float64), axis, -1)
    blocks = v.reshape(v.shape[:-1] + (-1, 32))
    amax = np.abs(blocks).max(-1, keepdims=True)
    byte = np.maximum(np.where(amax > 0, np.frexp(amax)[1] - 1 + 127, 0) - down, 1)
    scale = np.exp2(byte - 127.0)
    codes = (blocks / scale).astype(np.float32).astype(dtype).astype(np.float64)
    return np.moveaxis((codes * scale).reshape(v.shape), -1, axis)


WIDE = False


def mx_kscale(k):
    if not WIDE:
        return np.ones(k)
    levels = np.array([10, -10, 5, -5, 0])
    a = np.random.permutation(np.resize(levels, k // 512 * 4)).reshape(k // 512, 4)
    idx = np.arange(k)
    return np.exp2(a[idx // 512, idx % 128 // 32])


BF16 = ml_dtypes.bfloat16


def bf(x):
    return np.asarray(x, np.float32).astype(BF16)


def f64(x):
    return np.asarray(x).astype(np.float64)


B, S, D, H, HD, FF = 1, 512, 2048, 16, 128, 8192
EPS = 1e-05


def layer_norm(x, scale, bias):
    mu = x.mean(-1, keepdims=True)
    var = x.var(-1, keepdims=True)
    return (x - mu) / np.sqrt(var + EPS) * scale + bias


def setup_inputs():
    s = mx_kscale(D)
    return {
        "x": bf(np.random.standard_normal((B, S, D)) + 0.5 * np.random.standard_normal((B, S, 1))),
        "ln1_s": bf((1.0 + 0.1 * np.random.standard_normal(D)) * s),
        "ln1_b": bf(0.1 * np.random.standard_normal(D) * s),
        "wq_k": bf(np.random.standard_normal((D, H, HD)) / np.sqrt(D) / s[:, None, None]),
        "wq_b": bf(0.1 * np.random.standard_normal((H, HD))),
        "wk_k": bf(np.random.standard_normal((D, HD)) / np.sqrt(D) / s[:, None]),
        "wk_b": bf(0.1 * np.random.standard_normal(HD)),
        "wv_k": bf(np.random.standard_normal((D, HD)) / np.sqrt(D) / s[:, None]),
        "wv_b": bf(0.1 * np.random.standard_normal(HD)),
    }


def reference(x, ln1_s, ln1_b, wq_k, wq_b, wk_k, wk_b, wv_k, wv_b):
    h = layer_norm(f64(x), f64(ln1_s), f64(ln1_b))
    hq = mxq(h, 2, "e4m3")
    q = (hq @ mxq(f64(wq_k).reshape(D, H * HD), 0, "e4m3")).reshape(B, S, H, HD) + f64(wq_b)
    k = (hq @ mxq(f64(wk_k), 0, "e4m3")) + f64(wk_b)
    v = (hq @ mxq(f64(wv_k), 0, "e4m3")) + f64(wv_b)
    return q, k, v

@@ -1,0 +1,198 @@
+from contextlib import ExitStack
+
+import concourse.mybir as mybir
+from concourse.masks import make_identity
+
+F32 = mybir.dt.float32
+BF16 = mybir.dt.bfloat16
+U32 = mybir.dt.uint32
+U8 = mybir.dt.uint8
+FP8X4 = mybir.dt.float8_e4m3fn_x4
+ALU = mybir.AluOpType
+ACT = mybir.ActivationFunctionType
+
+P = 128
+PACK = 4
+TOKENS = 512
+D = 2048
+Q_COLS = 2048
+HEAD = 128
+EPS = 1e-05
+
+TOKEN_TILES = TOKENS // P
+D_SQUARES = D // P
+PASSES = D // (P * PACK)
+BANK = 512
+BANKS = 8
+STATS_CHUNK = 512
+LOAD_COLS = 1024
+RUN = 4
+
+FLOPS = 2 * TOKENS * D * (Q_COLS + 2 * HEAD)
+
+
+def quantise_rows(nc, stage, copy, rows, codes, scales):
+    width = rows.shape[2]
+    grouped = stage.tile([P, BANK, PACK], BF16, align_bytes=64, tag="grouped")
+    copy(
+        out=grouped[:, :width, :].rearrange("p (c i) t -> p c t i", i=RUN),
+        in_=rows.rearrange("p t (c i) -> p c t i", i=RUN),
+    )
+    nc.vector.quantize_mx(
+        out=codes.bitcast(FP8X4),
+        scales=scales,
+        in_=grouped[:, :width, :].rearrange("p w t -> p (w t)"),
+    )
+
+
+def tile_transformerlayer_pa_kernel(
+    tc, x, ln1_s, ln1_b, wq_k, wq_b, wk_k, wk_b, wv_k, wv_b, out_0, out_1, out_2
+):
+    nc = tc.nc
+
+    x_tiles = x.rearrange("b (i p) d -> (b i) p d", p=P)
+    wq_rows = wq_k.rearrange("(j p) h e -> p j (h e)", p=P)
+    wk_rows = wk_k.rearrange("(j p) e -> p j e", p=P)
+    wv_rows = wv_k.rearrange("(j p) e -> p j e", p=P)
+    q_tiles = out_0.rearrange("b (i p) h e -> (b i) p (h e)", p=P)
+    k_tiles = out_1.rearrange("b (i p) e -> (b i) p e", p=P)
+    v_tiles = out_2.rearrange("b (i p) e -> (b i) p e", p=P)
+
+    with ExitStack() as ctx:
+        keep = ctx.enter_context(tc.tile_pool(name="keep", bufs=1))
+        small = ctx.enter_context(tc.tile_pool(name="small", bufs=TOKEN_TILES))
+        stage = ctx.enter_context(tc.tile_pool(name="stage", bufs=4))
+        quantised = ctx.enter_context(tc.tile_pool(name="quantised", bufs=3))
+        results = ctx.enter_context(tc.tile_pool(name="results", bufs=6))
+        psum = ctx.enter_context(tc.psum_pool(name="psum", bufs=BANKS))
+
+        identity = keep.tile([P, P], F32, name="identity")
+        make_identity(nc, identity[:])
+        minus_half = keep.tile([P, 1], F32, name="minus_half")
+        nc.vector.memset(minus_half[:], -0.5)
+
+        x_sb = []
+        for i in range(TOKEN_TILES):
+            x_i = keep.tile([P, D], BF16, name="x%d" % i)
+            nc.sync.dma_start(out=x_i[:], in_=x_tiles[i])
+            x_sb.append(x_i)
+
+        gain_rows = keep.tile([P, P], BF16, name="gain_rows")
+        nc.vector.memset(gain_rows[:], 0.0)
+        nc.scalar.dma_start(out=gain_rows[0:D_SQUARES, :], in_=ln1_s.rearrange("(j p) -> j p", p=P))
+        nc.scalar.dma_start(
+            out=gain_rows[D_SQUARES : 2 * D_SQUARES, :], in_=ln1_b.rearrange("(j p) -> j p", p=P)
+        )
+
+        bias_all = keep.tile([P, Q_COLS + 2 * HEAD], BF16, name="bias_all")
+        wq_sb = {}
+        for half in range(Q_COLS // LOAD_COLS):
+            for g in range(PASSES):
+                w_hg = keep.tile([P, PACK, LOAD_COLS], BF16, name="wq%d_%d" % (half, g))
+                nc.sync.dma_start(
+                    out=w_hg[:],
+                    in_=wq_rows[:, PACK * g : PACK * (g + 1), LOAD_COLS * half : LOAD_COLS * (half + 1)],
+                )
+                wq_sb[(half, g)] = w_hg
+            if half == 0:
+                nc.sync.dma_start(
+                    out=bias_all[:, 0:Q_COLS], in_=wq_b.rearrange("h e -> (h e)").partition_broadcast(P)
+                )
+                nc.sync.dma_start(out=bias_all[:, Q_COLS : Q_COLS + HEAD], in_=wk_b.partition_broadcast(P))
+                nc.sync.dma_start(out=bias_all[:, Q_COLS + HEAD :], in_=wv_b.partition_broadcast(P))
+        wkv_sb = keep.tile([P, D_SQUARES, 2 * HEAD], BF16, name="wkv")
+        nc.sync.dma_start(out=wkv_sb[:, :, 0:HEAD], in_=wk_rows)
+        nc.sync.dma_start(out=wkv_sb[:, :, HEAD:], in_=wv_rows)
+
+        gain_rows_f32 = keep.tile([P, P], F32, name="gain_rows_f32")
+        nc.vector.tensor_copy(out=gain_rows_f32[:], in_=gain_rows[:])
+        gain_bank = psum.tile([P, BANK], F32, tag="bank", name="gain_bank")
+        nc.tensor.transpose(gain_bank[:, 0:P], gain_rows_f32[:], identity[:])
+        gain_cols = keep.tile([P, 2 * D_SQUARES], F32, name="gain_cols")
+        nc.vector.tensor_copy(out=gain_cols[:], in_=gain_bank[:, 0 : 2 * D_SQUARES])
+
+        normed = []
+        for i in range(TOKEN_TILES):
+            stats = small.tile([P, D // STATS_CHUNK, 6], F32, name="stats")
+            for c in range(D // STATS_CHUNK):
+                nc.vector.bn_stats(
+                    out=stats[:, c, :], in_=x_sb[i][:, STATS_CHUNK * c : STATS_CHUNK * (c + 1)]
+                )
+            mean_var = small.tile([P, 2], F32, name="mean_var")
+            nc.vector.bn_aggr(out=mean_var[:], in_=stats[:].rearrange("p c s -> p (c s)"))
+            var_eps = small.tile([P, 1], F32, name="var_eps")
+            nc.vector.tensor_scalar_add(out=var_eps[:], in0=mean_var[:, 1:2], scalar1=EPS)
+            rstd = small.tile([P, 1], F32, name="rstd")
+            nc.gpsimd.tensor_tensor(out=rstd[:], in0=var_eps[:], in1=minus_half[:], op=ALU.pow)
+            shift = small.tile([P, 1], F32, name="shift")
+            nc.vector.tensor_scalar(
+                out=shift[:], in0=mean_var[:, 0:1], scalar1=rstd[:], scalar2=-1.0, op0=ALU.mult, op1=ALU.mult
+            )
+            normed_i = keep.tile([P, D], F32, name="normed%d" % i)
+            nc.scalar.activation(out=normed_i[:], in_=x_sb[i][:], func=ACT.Identity, scale=rstd[:], bias=shift[:])
+            normed.append(normed_i)
+
+        h_rows = keep.tile([P, D_SQUARES, TOKENS], BF16, name="h_rows")
+        for j in range(D_SQUARES):
+            square = psum.tile([P, BANK], F32, tag="bank", name="square")
+            for i in range(TOKEN_TILES):
+                nc.tensor.transpose(square[:, P * i : P * (i + 1)], normed[i][:, P * j : P * (j + 1)], identity[:])
+            nc.scalar.activation(
+                out=h_rows[:, j, :],
+                in_=square[:],
+                func=ACT.Identity,
+                scale=gain_cols[:, j : j + 1],
+                bias=gain_cols[:, D_SQUARES + j : D_SQUARES + j + 1],
+            )
+
+        h_codes = keep.tile([P, PASSES, TOKENS], U32, name="h_codes", align_bytes=64)
+        h_scales = keep.tile([P, PASSES, TOKENS], U8, name="h_scales", align_bytes=64)
+        for g in range(PASSES):
+            quantise_rows(
+                nc,
+                stage,
+                nc.vector.tensor_copy,
+                h_rows[:, PACK * g : PACK * (g + 1), :],
+                h_codes[:, g, :],
+                h_scales[:, g, :],
+            )
+
+        blocks = []
+        for b in range(Q_COLS // BANK):
+            half, part = divmod(b, LOAD_COLS // BANK)
+            blocks.append([wq_sb[(half, g)][:, :, BANK * part : BANK * (part + 1)] for g in range(PASSES)])
+        blocks.append([wkv_sb[:, PACK * g : PACK * (g + 1), :] for g in range(PASSES)])
+
+        units = 0
+        for b, block in enumerate(blocks):
+            width = block[0].shape[2]
+            w_codes = quantised.tile([P, PASSES, BANK], U32, name="w_codes", align_bytes=64)
+            w_scales = quantised.tile([P, PASSES, BANK], U8, name="w_scales", align_bytes=64)
+            sums = [psum.tile([P, BANK], F32, tag="bank", name="sums%d" % i) for i in range(TOKEN_TILES)]
+            for g in range(PASSES):
+                copy = nc.vector.tensor_copy if units % 3 == 0 else nc.scalar.copy
+                units += 1
+                quantise_rows(nc, stage, copy, block[g], w_codes[:, g, :width], w_scales[:, g, :width])
+                for i in range(TOKEN_TILES):
+                    nc.tensor.matmul_mx(
+                        out=sums[i][:, :width],
+                        lhsT=h_codes[:, g, P * i : P * (i + 1)].bitcast(FP8X4),
+                        lhsT_scale=h_scales[:, g, P * i : P * (i + 1)],
+                        rhs=w_codes[:, g, :width].bitcast(FP8X4),
+                        rhs_scale=w_scales[:, g, :width],
+                        start=(g == 0),
+                        stop=(g == PASSES - 1),
+                    )
+            for i in range(TOKEN_TILES):
+                result = results.tile([P, BANK], F32, name="result")
+                nc.vector.tensor_tensor(
+                    out=result[:, :width],
+                    in0=sums[i][:, :width],
+                    in1=bias_all[:, BANK * b : BANK * b + width],
+                    op=ALU.add,
+                )
+                if b < Q_COLS // BANK:
+                    nc.sync.dma_start(out=q_tiles[i][:, BANK * b : BANK * (b + 1)], in_=result[:])
+                else:
+                    nc.sync.dma_start(out=k_tiles[i], in_=result[:, 0:HEAD])
+                    nc.sync.dma_start(out=v_tiles[i], in_=result[:, HEAD : 2 * HEAD])

@@ -25,24 +25,18 @@ PASSES = D // (P * PACK)
 BANK = 512
 BANKS = 8
 STATS_CHUNK = 512
-LOAD_COLS = 1024
 RUN = 4
 
+Q_BLOCKS = Q_COLS // BANK
+BLOCKS = Q_BLOCKS + 1
+PIECES = BLOCKS * PASSES
+EARLY_SCALAR = 5
+EARLY_PIECES = 2 * PASSES
+AHEAD = 2
+GROUPED_BUFS = 8
+BIAS_AFTER_PIECE = 12
+
 FLOPS = 2 * TOKENS * D * (Q_COLS + 2 * HEAD)
-
-
-def quantise_rows(nc, stage, copy, rows, codes, scales):
-    width = rows.shape[2]
-    grouped = stage.tile([P, BANK, PACK], BF16, align_bytes=64, tag="grouped")
-    copy(
-        out=grouped[:, :width, :].rearrange("p (c i) t -> p c t i", i=RUN),
-        in_=rows.rearrange("p t (c i) -> p c t i", i=RUN),
-    )
-    nc.vector.quantize_mx(
-        out=codes.bitcast(FP8X4),
-        scales=scales,
-        in_=grouped[:, :width, :].rearrange("p w t -> p (w t)"),
-    )
 
 
 def tile_transformerlayer_pa_kernel(
@@ -59,9 +53,10 @@ def tile_transformerlayer_pa_kernel(
     v_tiles = out_2.rearrange("b (i p) e -> (b i) p e", p=P)
 
     with ExitStack() as ctx:
+        ctx.enter_context(tc.manual_schedule())
         keep = ctx.enter_context(tc.tile_pool(name="keep", bufs=1))
         small = ctx.enter_context(tc.tile_pool(name="small", bufs=TOKEN_TILES))
-        stage = ctx.enter_context(tc.tile_pool(name="stage", bufs=4))
+        stage = ctx.enter_context(tc.tile_pool(name="stage", bufs=GROUPED_BUFS))
         quantised = ctx.enter_context(tc.tile_pool(name="quantised", bufs=3))
         results = ctx.enter_context(tc.tile_pool(name="results", bufs=6))
         psum = ctx.enter_context(tc.psum_pool(name="psum", bufs=BANKS))
@@ -71,45 +66,76 @@ def tile_transformerlayer_pa_kernel(
         minus_half = keep.tile([P, 1], F32, name="minus_half")
         nc.vector.memset(minus_half[:], -0.5)
 
+        gain_rows = keep.tile([P, P], BF16, name="gain_rows")
+        nc.vector.memset(gain_rows[2 * D_SQUARES : 4 * D_SQUARES, :], 0.0)
+        nc.vector.memset(gain_rows[4 * D_SQUARES :, :], 0.0)
+        nc.scalar.dma_start(out=gain_rows[0:D_SQUARES, :], in_=ln1_s.rearrange("(j p) -> j p", p=P))
+        nc.scalar.dma_start(
+            out=gain_rows[D_SQUARES : 2 * D_SQUARES, :], in_=ln1_b.rearrange("(j p) -> j p", p=P)
+        )
+        gain_rows_f32 = keep.tile([P, P], F32, name="gain_rows_f32")
+        nc.scalar.copy(out=gain_rows_f32[:], in_=gain_rows[:])
+        gain_bank = psum.tile([P, BANK], F32, tag="bank", name="gain_bank")
+        nc.tensor.transpose(gain_bank[:, 0:P], gain_rows_f32[:], identity[:])
+        gain_cols = keep.tile([P, 2 * D_SQUARES], F32, name="gain_cols")
+        nc.scalar.copy(out=gain_cols[:], in_=gain_bank[:, 0 : 2 * D_SQUARES])
+
+        piece_rows = []
+
+        def load_piece():
+            b, g = divmod(len(piece_rows), PASSES)
+            squares = slice(PACK * g, PACK * (g + 1))
+            if b < Q_BLOCKS:
+                rows = keep.tile([P, PACK, BANK], BF16, name="w%d_%d" % (b, g))
+                nc.sync.dma_start(out=rows[:], in_=wq_rows[:, squares, BANK * b : BANK * (b + 1)])
+            else:
+                rows = keep.tile([P, PACK, 2 * HEAD], BF16, name="wkv%d" % g)
+                nc.sync.dma_start(out=rows[:, :, 0:HEAD], in_=wk_rows[:, squares, :])
+                nc.sync.dma_start(out=rows[:, :, HEAD:], in_=wv_rows[:, squares, :])
+            piece_rows.append(rows)
+
         x_sb = []
         for i in range(TOKEN_TILES):
             x_i = keep.tile([P, D], BF16, name="x%d" % i)
             nc.sync.dma_start(out=x_i[:], in_=x_tiles[i])
             x_sb.append(x_i)
-
-        gain_rows = keep.tile([P, P], BF16, name="gain_rows")
-        nc.vector.memset(gain_rows[:], 0.0)
-        nc.scalar.dma_start(out=gain_rows[0:D_SQUARES, :], in_=ln1_s.rearrange("(j p) -> j p", p=P))
-        nc.scalar.dma_start(
-            out=gain_rows[D_SQUARES : 2 * D_SQUARES, :], in_=ln1_b.rearrange("(j p) -> j p", p=P)
-        )
-
+            load_piece()
         bias_all = keep.tile([P, Q_COLS + 2 * HEAD], BF16, name="bias_all")
-        wq_sb = {}
-        for half in range(Q_COLS // LOAD_COLS):
-            for g in range(PASSES):
-                w_hg = keep.tile([P, PACK, LOAD_COLS], BF16, name="wq%d_%d" % (half, g))
-                nc.sync.dma_start(
-                    out=w_hg[:],
-                    in_=wq_rows[:, PACK * g : PACK * (g + 1), LOAD_COLS * half : LOAD_COLS * (half + 1)],
-                )
-                wq_sb[(half, g)] = w_hg
-            if half == 0:
+        for u in range(TOKEN_TILES, PIECES):
+            load_piece()
+            if u == BIAS_AFTER_PIECE:
                 nc.sync.dma_start(
                     out=bias_all[:, 0:Q_COLS], in_=wq_b.rearrange("h e -> (h e)").partition_broadcast(P)
                 )
                 nc.sync.dma_start(out=bias_all[:, Q_COLS : Q_COLS + HEAD], in_=wk_b.partition_broadcast(P))
                 nc.sync.dma_start(out=bias_all[:, Q_COLS + HEAD :], in_=wv_b.partition_broadcast(P))
-        wkv_sb = keep.tile([P, D_SQUARES, 2 * HEAD], BF16, name="wkv")
-        nc.sync.dma_start(out=wkv_sb[:, :, 0:HEAD], in_=wk_rows)
-        nc.sync.dma_start(out=wkv_sb[:, :, HEAD:], in_=wv_rows)
 
-        gain_rows_f32 = keep.tile([P, P], F32, name="gain_rows_f32")
-        nc.vector.tensor_copy(out=gain_rows_f32[:], in_=gain_rows[:])
-        gain_bank = psum.tile([P, BANK], F32, tag="bank", name="gain_bank")
-        nc.tensor.transpose(gain_bank[:, 0:P], gain_rows_f32[:], identity[:])
-        gain_cols = keep.tile([P, 2 * D_SQUARES], F32, name="gain_cols")
-        nc.vector.tensor_copy(out=gain_cols[:], in_=gain_bank[:, 0 : 2 * D_SQUARES])
+        def regroup(copy, rows):
+            width = rows.shape[2]
+            grouped = stage.tile([P, BANK, PACK], BF16, align_bytes=64, name="grouped")
+            copy(
+                out=grouped[:, :width, :].rearrange("p (c i) t -> p c t i", i=RUN),
+                in_=rows.rearrange("p t (c i) -> p c t i", i=RUN),
+            )
+            return grouped[:, :width, :].rearrange("p w t -> p (w t)")
+
+        def quantise(grouped, codes, scales):
+            nc.vector.quantize_mx(out=codes.bitcast(FP8X4), scales=scales, in_=grouped)
+
+        piece_grouped = {}
+        block_codes = {}
+        block_scales = {}
+
+        def regroup_piece(u, copy):
+            piece_grouped[u] = regroup(copy, piece_rows[u][:])
+
+        def quantise_piece(u):
+            b, g = divmod(u, PASSES)
+            if g == 0:
+                block_codes[b] = quantised.tile([P, PASSES, BANK], U32, name="w_codes", align_bytes=64)
+                block_scales[b] = quantised.tile([P, PASSES, BANK], U8, name="w_scales", align_bytes=64)
+            width = piece_rows[u].shape[2]
+            quantise(piece_grouped[u], block_codes[b][:, g, :width], block_scales[b][:, g, :width])
 
         normed = []
         for i in range(TOKEN_TILES):
@@ -122,77 +148,94 @@ def tile_transformerlayer_pa_kernel(
             nc.vector.bn_aggr(out=mean_var[:], in_=stats[:].rearrange("p c s -> p (c s)"))
             var_eps = small.tile([P, 1], F32, name="var_eps")
             nc.vector.tensor_scalar_add(out=var_eps[:], in0=mean_var[:, 1:2], scalar1=EPS)
+            minus_mean = small.tile([P, 1], F32, name="minus_mean")
+            nc.vector.tensor_scalar_mul(out=minus_mean[:], in0=mean_var[:, 0:1], scalar1=-1.0)
             rstd = small.tile([P, 1], F32, name="rstd")
             nc.gpsimd.tensor_tensor(out=rstd[:], in0=var_eps[:], in1=minus_half[:], op=ALU.pow)
-            shift = small.tile([P, 1], F32, name="shift")
-            nc.vector.tensor_scalar(
-                out=shift[:], in0=mean_var[:, 0:1], scalar1=rstd[:], scalar2=-1.0, op0=ALU.mult, op1=ALU.mult
-            )
             normed_i = keep.tile([P, D], F32, name="normed%d" % i)
-            nc.scalar.activation(out=normed_i[:], in_=x_sb[i][:], func=ACT.Identity, scale=rstd[:], bias=shift[:])
+            nc.gpsimd.tensor_scalar(
+                out=normed_i[:],
+                in0=x_sb[i][:],
+                scalar1=minus_mean[:],
+                scalar2=rstd[:],
+                op0=ALU.add,
+                op1=ALU.mult,
+            )
             normed.append(normed_i)
 
-        h_rows = keep.tile([P, D_SQUARES, TOKENS], BF16, name="h_rows")
-        for j in range(D_SQUARES):
-            square = psum.tile([P, BANK], F32, tag="bank", name="square")
-            for i in range(TOKEN_TILES):
-                nc.tensor.transpose(square[:, P * i : P * (i + 1)], normed[i][:, P * j : P * (j + 1)], identity[:])
-            nc.scalar.activation(
-                out=h_rows[:, j, :],
-                in_=square[:],
-                func=ACT.Identity,
-                scale=gain_cols[:, j : j + 1],
-                bias=gain_cols[:, D_SQUARES + j : D_SQUARES + j + 1],
-            )
+        for u in range(EARLY_SCALAR):
+            regroup_piece(u, nc.scalar.copy)
+        for u in range(EARLY_SCALAR):
+            quantise_piece(u)
+        for u in range(EARLY_SCALAR, EARLY_PIECES):
+            regroup_piece(u, nc.vector.tensor_copy)
+        for u in range(EARLY_SCALAR, EARLY_PIECES):
+            quantise_piece(u)
 
+        h_rows = keep.tile([P, D_SQUARES, TOKENS], BF16, name="h_rows")
         h_codes = keep.tile([P, PASSES, TOKENS], U32, name="h_codes", align_bytes=64)
         h_scales = keep.tile([P, PASSES, TOKENS], U8, name="h_scales", align_bytes=64)
         for g in range(PASSES):
-            quantise_rows(
-                nc,
-                stage,
-                nc.vector.tensor_copy,
-                h_rows[:, PACK * g : PACK * (g + 1), :],
-                h_codes[:, g, :],
-                h_scales[:, g, :],
-            )
-
-        blocks = []
-        for b in range(Q_COLS // BANK):
-            half, part = divmod(b, LOAD_COLS // BANK)
-            blocks.append([wq_sb[(half, g)][:, :, BANK * part : BANK * (part + 1)] for g in range(PASSES)])
-        blocks.append([wkv_sb[:, PACK * g : PACK * (g + 1), :] for g in range(PASSES)])
-
-        units = 0
-        for b, block in enumerate(blocks):
-            width = block[0].shape[2]
-            w_codes = quantised.tile([P, PASSES, BANK], U32, name="w_codes", align_bytes=64)
-            w_scales = quantised.tile([P, PASSES, BANK], U8, name="w_scales", align_bytes=64)
-            sums = [psum.tile([P, BANK], F32, tag="bank", name="sums%d" % i) for i in range(TOKEN_TILES)]
-            for g in range(PASSES):
-                copy = nc.vector.tensor_copy if units % 3 == 0 else nc.scalar.copy
-                units += 1
-                quantise_rows(nc, stage, copy, block[g], w_codes[:, g, :width], w_scales[:, g, :width])
+            for j in range(PACK * g, PACK * (g + 1)):
+                square = psum.tile([P, BANK], F32, tag="bank", name="square")
                 for i in range(TOKEN_TILES):
-                    nc.tensor.matmul_mx(
-                        out=sums[i][:, :width],
-                        lhsT=h_codes[:, g, P * i : P * (i + 1)].bitcast(FP8X4),
-                        lhsT_scale=h_scales[:, g, P * i : P * (i + 1)],
-                        rhs=w_codes[:, g, :width].bitcast(FP8X4),
-                        rhs_scale=w_scales[:, g, :width],
-                        start=(g == 0),
-                        stop=(g == PASSES - 1),
+                    nc.tensor.transpose(
+                        square[:, P * i : P * (i + 1)], normed[i][:, P * j : P * (j + 1)], identity[:]
                     )
+                nc.scalar.activation(
+                    out=h_rows[:, j, :],
+                    in_=square[:],
+                    func=ACT.Identity,
+                    scale=gain_cols[:, j : j + 1],
+                    bias=gain_cols[:, D_SQUARES + j : D_SQUARES + j + 1],
+                )
+            h_grouped = regroup(nc.vector.tensor_copy, h_rows[:, PACK * g : PACK * (g + 1), :])
+            quantise(h_grouped, h_codes[:, g, :], h_scales[:, g, :])
+
+        block_sums = {}
+
+        def multiply_piece(u):
+            b, g = divmod(u, PASSES)
+            width = piece_rows[u].shape[2]
+            if g == 0:
+                block_sums[b] = [
+                    psum.tile([P, BANK], F32, tag="bank", name="sums%d" % i) for i in range(TOKEN_TILES)
+                ]
+            for i in range(TOKEN_TILES):
+                nc.tensor.matmul_mx(
+                    out=block_sums[b][i][:, :width],
+                    lhsT=h_codes[:, g, P * i : P * (i + 1)].bitcast(FP8X4),
+                    lhsT_scale=h_scales[:, g, P * i : P * (i + 1)],
+                    rhs=block_codes[b][:, g, :width].bitcast(FP8X4),
+                    rhs_scale=block_scales[b][:, g, :width],
+                    start=(g == 0),
+                    stop=(g == PASSES - 1),
+                )
+
+        def finish_block(b):
+            width = piece_rows[PASSES * b].shape[2]
             for i in range(TOKEN_TILES):
                 result = results.tile([P, BANK], F32, name="result")
                 nc.vector.tensor_tensor(
                     out=result[:, :width],
-                    in0=sums[i][:, :width],
+                    in0=block_sums[b][i][:, :width],
                     in1=bias_all[:, BANK * b : BANK * b + width],
                     op=ALU.add,
                 )
-                if b < Q_COLS // BANK:
+                if b < Q_BLOCKS:
                     nc.sync.dma_start(out=q_tiles[i][:, BANK * b : BANK * (b + 1)], in_=result[:])
                 else:
                     nc.sync.dma_start(out=k_tiles[i], in_=result[:, 0:HEAD])
                     nc.sync.dma_start(out=v_tiles[i], in_=result[:, HEAD : 2 * HEAD])
+
+        for u in range(PIECES):
+            b, g = divmod(u, PASSES)
+            ahead = u + AHEAD
+            if EARLY_PIECES <= ahead < PIECES:
+                regroup_piece(ahead, nc.vector.tensor_copy if ahead % PASSES == 0 else nc.scalar.copy)
+            if u >= EARLY_PIECES:
+                quantise_piece(u)
+            multiply_piece(u)
+            if g == 2 and b > 0:
+                finish_block(b - 1)
+        finish_block(BLOCKS - 1)

@@ -25,15 +25,17 @@ PASSES = D // (P * PACK)
 BANK = 512
 BANKS = 8
 STATS_CHUNK = 512
+CHUNKS = D // STATS_CHUNK
 RUN = 4
 
 Q_BLOCKS = Q_COLS // BANK
 BLOCKS = Q_BLOCKS + 1
 PIECES = BLOCKS * PASSES
-EARLY_SCALAR = 5
+EARLY_SCALAR = PASSES
 EARLY_PIECES = 2 * PASSES
 AHEAD = 2
 GROUPED_BUFS = 8
+LOADED_BUFS = 12
 BIAS_AFTER_PIECE = 12
 
 FLOPS = 2 * TOKENS * D * (Q_COLS + 2 * HEAD)
@@ -56,7 +58,9 @@ def tile_transformerlayer_pa_kernel(
         ctx.enter_context(tc.manual_schedule())
         keep = ctx.enter_context(tc.tile_pool(name="keep", bufs=1))
         small = ctx.enter_context(tc.tile_pool(name="small", bufs=TOKEN_TILES))
+        loaded = ctx.enter_context(tc.tile_pool(name="loaded", bufs=LOADED_BUFS))
         stage = ctx.enter_context(tc.tile_pool(name="stage", bufs=GROUPED_BUFS))
+        h_stage = ctx.enter_context(tc.tile_pool(name="h_stage", bufs=2))
         quantised = ctx.enter_context(tc.tile_pool(name="quantised", bufs=3))
         results = ctx.enter_context(tc.tile_pool(name="results", bufs=6))
         psum = ctx.enter_context(tc.psum_pool(name="psum", bufs=BANKS))
@@ -85,14 +89,14 @@ def tile_transformerlayer_pa_kernel(
         def load_piece():
             b, g = divmod(len(piece_rows), PASSES)
             squares = slice(PACK * g, PACK * (g + 1))
+            rows = loaded.tile([P, PACK, BANK], BF16, name="rows")
             if b < Q_BLOCKS:
-                rows = keep.tile([P, PACK, BANK], BF16, name="w%d_%d" % (b, g))
                 nc.sync.dma_start(out=rows[:], in_=wq_rows[:, squares, BANK * b : BANK * (b + 1)])
+                piece_rows.append(rows[:])
             else:
-                rows = keep.tile([P, PACK, 2 * HEAD], BF16, name="wkv%d" % g)
                 nc.sync.dma_start(out=rows[:, :, 0:HEAD], in_=wk_rows[:, squares, :])
-                nc.sync.dma_start(out=rows[:, :, HEAD:], in_=wv_rows[:, squares, :])
-            piece_rows.append(rows)
+                nc.sync.dma_start(out=rows[:, :, HEAD : 2 * HEAD], in_=wv_rows[:, squares, :])
+                piece_rows.append(rows[:, :, 0 : 2 * HEAD])
 
         x_sb = []
         for i in range(TOKEN_TILES):
@@ -110,9 +114,9 @@ def tile_transformerlayer_pa_kernel(
                 nc.sync.dma_start(out=bias_all[:, Q_COLS : Q_COLS + HEAD], in_=wk_b.partition_broadcast(P))
                 nc.sync.dma_start(out=bias_all[:, Q_COLS + HEAD :], in_=wv_b.partition_broadcast(P))
 
-        def regroup(copy, rows):
+        def regroup(pool, copy, rows):
             width = rows.shape[2]
-            grouped = stage.tile([P, BANK, PACK], BF16, align_bytes=64, name="grouped")
+            grouped = pool.tile([P, BANK, PACK], BF16, align_bytes=64, name="grouped")
             copy(
                 out=grouped[:, :width, :].rearrange("p (c i) t -> p c t i", i=RUN),
                 in_=rows.rearrange("p t (c i) -> p c t i", i=RUN),
@@ -127,7 +131,7 @@ def tile_transformerlayer_pa_kernel(
         block_scales = {}
 
         def regroup_piece(u, copy):
-            piece_grouped[u] = regroup(copy, piece_rows[u][:])
+            piece_grouped[u] = regroup(stage, copy, piece_rows[u])
 
         def quantise_piece(u):
             b, g = divmod(u, PASSES)
@@ -137,36 +141,47 @@ def tile_transformerlayer_pa_kernel(
             width = piece_rows[u].shape[2]
             quantise(piece_grouped[u], block_codes[b][:, g, :width], block_scales[b][:, g, :width])
 
-        normed = []
-        for i in range(TOKEN_TILES):
-            stats = small.tile([P, D // STATS_CHUNK, 6], F32, name="stats")
-            for c in range(D // STATS_CHUNK):
-                nc.vector.bn_stats(
-                    out=stats[:, c, :], in_=x_sb[i][:, STATS_CHUNK * c : STATS_CHUNK * (c + 1)]
-                )
-            mean_var = small.tile([P, 2], F32, name="mean_var")
-            nc.vector.bn_aggr(out=mean_var[:], in_=stats[:].rearrange("p c s -> p (c s)"))
-            var_eps = small.tile([P, 1], F32, name="var_eps")
-            nc.vector.tensor_scalar_add(out=var_eps[:], in0=mean_var[:, 1:2], scalar1=EPS)
-            minus_mean = small.tile([P, 1], F32, name="minus_mean")
-            nc.vector.tensor_scalar_mul(out=minus_mean[:], in0=mean_var[:, 0:1], scalar1=-1.0)
-            rstd = small.tile([P, 1], F32, name="rstd")
-            nc.gpsimd.tensor_tensor(out=rstd[:], in0=var_eps[:], in1=minus_half[:], op=ALU.pow)
-            normed_i = keep.tile([P, D], F32, name="normed%d" % i)
-            nc.gpsimd.tensor_scalar(
-                out=normed_i[:],
-                in0=x_sb[i][:],
-                scalar1=minus_mean[:],
-                scalar2=rstd[:],
-                op0=ALU.add,
-                op1=ALU.mult,
-            )
-            normed.append(normed_i)
-
         for u in range(EARLY_SCALAR):
             regroup_piece(u, nc.scalar.copy)
-        for u in range(EARLY_SCALAR):
-            quantise_piece(u)
+
+        stats = [small.tile([P, CHUNKS, 6], F32, name="stats") for i in range(TOKEN_TILES)]
+        mean_var = [small.tile([P, 2], F32, name="mean_var") for i in range(TOKEN_TILES)]
+        normed = [keep.tile([P, D], F32, name="normed%d" % i) for i in range(TOKEN_TILES)]
+
+        def normalise(i):
+            var_eps = small.tile([P, 1], F32, name="var_eps")
+            nc.vector.tensor_scalar_add(out=var_eps[:], in0=mean_var[i][:, 1:2], scalar1=EPS)
+            minus_mean = small.tile([P, 1], F32, name="minus_mean")
+            nc.vector.tensor_scalar_mul(out=minus_mean[:], in0=mean_var[i][:, 0:1], scalar1=-1.0)
+            rstd = small.tile([P, 1], F32, name="rstd")
+            nc.gpsimd.tensor_tensor(out=rstd[:], in0=var_eps[:], in1=minus_half[:], op=ALU.pow)
+            if i < TOKEN_TILES - 1:
+                nc.gpsimd.tensor_scalar(
+                    out=normed[i][:],
+                    in0=x_sb[i][:],
+                    scalar1=minus_mean[:],
+                    scalar2=rstd[:],
+                    op0=ALU.add,
+                    op1=ALU.mult,
+                )
+            else:
+                shift = small.tile([P, 1], F32, name="shift")
+                nc.vector.tensor_mul(out=shift[:], in0=minus_mean[:], in1=rstd[:])
+                nc.scalar.activation(
+                    out=normed[i][:], in_=x_sb[i][:], func=ACT.Identity, scale=rstd[:], bias=shift[:]
+                )
+
+        for i in range(TOKEN_TILES + 1):
+            for c in range(CHUNKS):
+                if i < TOKEN_TILES:
+                    nc.vector.bn_stats(
+                        out=stats[i][:, c, :], in_=x_sb[i][:, STATS_CHUNK * c : STATS_CHUNK * (c + 1)]
+                    )
+                if i > 0 and c == 0:
+                    nc.vector.bn_aggr(out=mean_var[i - 1][:], in_=stats[i - 1][:].rearrange("p c s -> p (c s)"))
+                if i > 0 and c == 1:
+                    normalise(i - 1)
+
         for u in range(EARLY_SCALAR, EARLY_PIECES):
             regroup_piece(u, nc.vector.tensor_copy)
         for u in range(EARLY_SCALAR, EARLY_PIECES):
@@ -189,7 +204,8 @@ def tile_transformerlayer_pa_kernel(
                     scale=gain_cols[:, j : j + 1],
                     bias=gain_cols[:, D_SQUARES + j : D_SQUARES + j + 1],
                 )
-            h_grouped = regroup(nc.vector.tensor_copy, h_rows[:, PACK * g : PACK * (g + 1), :])
+            h_grouped = regroup(h_stage, nc.vector.tensor_copy, h_rows[:, PACK * g : PACK * (g + 1), :])
+            quantise_piece(g)
             quantise(h_grouped, h_codes[:, g, :], h_scales[:, g, :])
 
         block_sums = {}

@@ -33,7 +33,6 @@ BLOCKS = Q_BLOCKS + 1
 PIECES = BLOCKS * PASSES
 EARLY_SCALAR = PASSES
 EARLY_PIECES = 2 * PASSES
-AHEAD = 2
 GROUPED_BUFS = 8
 LOADED_BUFS = 12
 BIAS_AFTER_PIECE = 12
@@ -60,7 +59,7 @@ def tile_transformerlayer_pa_kernel(
         small = ctx.enter_context(tc.tile_pool(name="small", bufs=TOKEN_TILES))
         loaded = ctx.enter_context(tc.tile_pool(name="loaded", bufs=LOADED_BUFS))
         stage = ctx.enter_context(tc.tile_pool(name="stage", bufs=GROUPED_BUFS))
-        h_stage = ctx.enter_context(tc.tile_pool(name="h_stage", bufs=2))
+        lone = ctx.enter_context(tc.tile_pool(name="lone", bufs=1))
         quantised = ctx.enter_context(tc.tile_pool(name="quantised", bufs=3))
         results = ctx.enter_context(tc.tile_pool(name="results", bufs=6))
         psum = ctx.enter_context(tc.psum_pool(name="psum", bufs=BANKS))
@@ -123,6 +122,9 @@ def tile_transformerlayer_pa_kernel(
             )
             return grouped[:, :width, :].rearrange("p w t -> p (w t)")
 
+        def gpsimd_copy(out, in_):
+            nc.gpsimd.tensor_scalar(out=out, in0=in_, scalar1=1.0, scalar2=0.0, op0=ALU.mult, op1=ALU.add)
+
         def quantise(grouped, codes, scales):
             nc.vector.quantize_mx(out=codes.bitcast(FP8X4), scales=scales, in_=grouped)
 
@@ -130,8 +132,8 @@ def tile_transformerlayer_pa_kernel(
         block_codes = {}
         block_scales = {}
 
-        def regroup_piece(u, copy):
-            piece_grouped[u] = regroup(stage, copy, piece_rows[u])
+        def regroup_piece(u, copy, pool=stage):
+            piece_grouped[u] = regroup(pool, copy, piece_rows[u])
 
         def quantise_piece(u):
             b, g = divmod(u, PASSES)
@@ -204,7 +206,7 @@ def tile_transformerlayer_pa_kernel(
                     scale=gain_cols[:, j : j + 1],
                     bias=gain_cols[:, D_SQUARES + j : D_SQUARES + j + 1],
                 )
-            h_grouped = regroup(h_stage, nc.vector.tensor_copy, h_rows[:, PACK * g : PACK * (g + 1), :])
+            h_grouped = regroup(lone, nc.vector.tensor_copy, h_rows[:, PACK * g : PACK * (g + 1), :])
             quantise_piece(g)
             quantise(h_grouped, h_codes[:, g, :], h_scales[:, g, :])
 
@@ -244,14 +246,16 @@ def tile_transformerlayer_pa_kernel(
                     nc.sync.dma_start(out=k_tiles[i], in_=result[:, 0:HEAD])
                     nc.sync.dma_start(out=v_tiles[i], in_=result[:, HEAD : 2 * HEAD])
 
-        for u in range(PIECES):
-            b, g = divmod(u, PASSES)
-            ahead = u + AHEAD
-            if EARLY_PIECES <= ahead < PIECES:
-                regroup_piece(ahead, nc.vector.tensor_copy if ahead % PASSES == 0 else nc.scalar.copy)
-            if u >= EARLY_PIECES:
-                quantise_piece(u)
+        for u in range(EARLY_PIECES):
             multiply_piece(u)
-            if g == 2 and b > 0:
-                finish_block(b - 1)
+
+        for b in range(2, BLOCKS):
+            regroup_piece(PASSES * b + PASSES - 1, gpsimd_copy, lone)
+            finish_block(b - 2)
+            for g in range(PASSES - 1):
+                regroup_piece(PASSES * b + g, nc.scalar.copy)
+            for g in range(PASSES):
+                quantise_piece(PASSES * b + g)
+                multiply_piece(PASSES * b + g)
+        finish_block(BLOCKS - 2)
         finish_block(BLOCKS - 1)

from contextlib import ExitStack

import concourse.mybir as mybir
from concourse.masks import make_identity

F32 = mybir.dt.float32
BF16 = mybir.dt.bfloat16
U32 = mybir.dt.uint32
U8 = mybir.dt.uint8
FP8X4 = mybir.dt.float8_e4m3fn_x4
ALU = mybir.AluOpType
ACT = mybir.ActivationFunctionType

P = 128
PACK = 4
TOKENS = 512
D = 2048
Q_COLS = 2048
HEAD = 128
EPS = 1e-05

TOKEN_TILES = TOKENS // P
D_SQUARES = D // P
PASSES = D // (P * PACK)
BANK = 512
BANKS = 8
STATS_CHUNK = 512
CHUNKS = D // STATS_CHUNK
RUN = 4

Q_BLOCKS = Q_COLS // BANK
BLOCKS = Q_BLOCKS + 1
PIECES = BLOCKS * PASSES
EARLY_SCALAR = PASSES
EARLY_PIECES = 2 * PASSES
GROUPED_BUFS = 8
LOADED_BUFS = 12
BIAS_AFTER_PIECE = 12

FLOPS = 2 * TOKENS * D * (Q_COLS + 2 * HEAD)


def tile_transformerlayer_pa_kernel(
    tc, x, ln1_s, ln1_b, wq_k, wq_b, wk_k, wk_b, wv_k, wv_b, out_0, out_1, out_2
):
    nc = tc.nc

    x_tiles = x.rearrange("b (i p) d -> (b i) p d", p=P)
    wq_rows = wq_k.rearrange("(j p) h e -> p j (h e)", p=P)
    wk_rows = wk_k.rearrange("(j p) e -> p j e", p=P)
    wv_rows = wv_k.rearrange("(j p) e -> p j e", p=P)
    q_tiles = out_0.rearrange("b (i p) h e -> (b i) p (h e)", p=P)
    k_tiles = out_1.rearrange("b (i p) e -> (b i) p e", p=P)
    v_tiles = out_2.rearrange("b (i p) e -> (b i) p e", p=P)

    with ExitStack() as ctx:
        ctx.enter_context(tc.manual_schedule())
        keep = ctx.enter_context(tc.tile_pool(name="keep", bufs=1))
        small = ctx.enter_context(tc.tile_pool(name="small", bufs=TOKEN_TILES))
        loaded = ctx.enter_context(tc.tile_pool(name="loaded", bufs=LOADED_BUFS))
        stage = ctx.enter_context(tc.tile_pool(name="stage", bufs=GROUPED_BUFS))
        lone = ctx.enter_context(tc.tile_pool(name="lone", bufs=1))
        quantised = ctx.enter_context(tc.tile_pool(name="quantised", bufs=3))
        results = ctx.enter_context(tc.tile_pool(name="results", bufs=6))
        psum = ctx.enter_context(tc.psum_pool(name="psum", bufs=BANKS))

        identity = keep.tile([P, P], F32, name="identity")
        make_identity(nc, identity[:])
        minus_half = keep.tile([P, 1], F32, name="minus_half")
        nc.vector.memset(minus_half[:], -0.5)

        gain_rows = keep.tile([P, P], BF16, name="gain_rows")
        nc.vector.memset(gain_rows[2 * D_SQUARES : 4 * D_SQUARES, :], 0.0)
        nc.vector.memset(gain_rows[4 * D_SQUARES :, :], 0.0)
        nc.scalar.dma_start(out=gain_rows[0:D_SQUARES, :], in_=ln1_s.rearrange("(j p) -> j p", p=P))
        nc.scalar.dma_start(
            out=gain_rows[D_SQUARES : 2 * D_SQUARES, :], in_=ln1_b.rearrange("(j p) -> j p", p=P)
        )
        gain_rows_f32 = keep.tile([P, P], F32, name="gain_rows_f32")
        nc.scalar.copy(out=gain_rows_f32[:], in_=gain_rows[:])
        gain_bank = psum.tile([P, BANK], F32, tag="bank", name="gain_bank")
        nc.tensor.transpose(gain_bank[:, 0:P], gain_rows_f32[:], identity[:])
        gain_cols = keep.tile([P, 2 * D_SQUARES], F32, name="gain_cols")
        nc.scalar.copy(out=gain_cols[:], in_=gain_bank[:, 0 : 2 * D_SQUARES])

        piece_rows = []

        def load_piece():
            b, g = divmod(len(piece_rows), PASSES)
            squares = slice(PACK * g, PACK * (g + 1))
            rows = loaded.tile([P, PACK, BANK], BF16, name="rows")
            if b < Q_BLOCKS:
                nc.sync.dma_start(out=rows[:], in_=wq_rows[:, squares, BANK * b : BANK * (b + 1)])
                piece_rows.append(rows[:])
            else:
                nc.sync.dma_start(out=rows[:, :, 0:HEAD], in_=wk_rows[:, squares, :])
                nc.sync.dma_start(out=rows[:, :, HEAD : 2 * HEAD], in_=wv_rows[:, squares, :])
                piece_rows.append(rows[:, :, 0 : 2 * HEAD])

        x_sb = []
        for i in range(TOKEN_TILES):
            x_i = keep.tile([P, D], BF16, name="x%d" % i)
            nc.sync.dma_start(out=x_i[:], in_=x_tiles[i])
            x_sb.append(x_i)
            load_piece()
        bias_all = keep.tile([P, Q_COLS + 2 * HEAD], BF16, name="bias_all")
        for u in range(TOKEN_TILES, PIECES):
            load_piece()
            if u == BIAS_AFTER_PIECE:
                nc.sync.dma_start(
                    out=bias_all[:, 0:Q_COLS], in_=wq_b.rearrange("h e -> (h e)").partition_broadcast(P)
                )
                nc.sync.dma_start(out=bias_all[:, Q_COLS : Q_COLS + HEAD], in_=wk_b.partition_broadcast(P))
                nc.sync.dma_start(out=bias_all[:, Q_COLS + HEAD :], in_=wv_b.partition_broadcast(P))

        def regroup(pool, copy, rows):
            width = rows.shape[2]
            grouped = pool.tile([P, BANK, PACK], BF16, align_bytes=64, name="grouped")
            copy(
                out=grouped[:, :width, :].rearrange("p (c i) t -> p c t i", i=RUN),
                in_=rows.rearrange("p t (c i) -> p c t i", i=RUN),
            )
            return grouped[:, :width, :].rearrange("p w t -> p (w t)")

        def gpsimd_copy(out, in_):
            nc.gpsimd.tensor_scalar(out=out, in0=in_, scalar1=1.0, scalar2=0.0, op0=ALU.mult, op1=ALU.add)

        def quantise(grouped, codes, scales):
            nc.vector.quantize_mx(out=codes.bitcast(FP8X4), scales=scales, in_=grouped)

        piece_grouped = {}
        block_codes = {}
        block_scales = {}

        def regroup_piece(u, copy, pool=stage):
            piece_grouped[u] = regroup(pool, copy, piece_rows[u])

        def quantise_piece(u):
            b, g = divmod(u, PASSES)
            if g == 0:
                block_codes[b] = quantised.tile([P, PASSES, BANK], U32, name="w_codes", align_bytes=64)
                block_scales[b] = quantised.tile([P, PASSES, BANK], U8, name="w_scales", align_bytes=64)
            width = piece_rows[u].shape[2]
            quantise(piece_grouped[u], block_codes[b][:, g, :width], block_scales[b][:, g, :width])

        for u in range(EARLY_SCALAR):
            regroup_piece(u, nc.scalar.copy)

        stats = [small.tile([P, CHUNKS, 6], F32, name="stats") for i in range(TOKEN_TILES)]
        mean_var = [small.tile([P, 2], F32, name="mean_var") for i in range(TOKEN_TILES)]
        normed = [keep.tile([P, D], F32, name="normed%d" % i) for i in range(TOKEN_TILES)]

        def normalise(i):
            var_eps = small.tile([P, 1], F32, name="var_eps")
            nc.vector.tensor_scalar_add(out=var_eps[:], in0=mean_var[i][:, 1:2], scalar1=EPS)
            minus_mean = small.tile([P, 1], F32, name="minus_mean")
            nc.vector.tensor_scalar_mul(out=minus_mean[:], in0=mean_var[i][:, 0:1], scalar1=-1.0)
            rstd = small.tile([P, 1], F32, name="rstd")
            nc.gpsimd.tensor_tensor(out=rstd[:], in0=var_eps[:], in1=minus_half[:], op=ALU.pow)
            if i < TOKEN_TILES - 1:
                nc.gpsimd.tensor_scalar(
                    out=normed[i][:],
                    in0=x_sb[i][:],
                    scalar1=minus_mean[:],
                    scalar2=rstd[:],
                    op0=ALU.add,
                    op1=ALU.mult,
                )
            else:
                shift = small.tile([P, 1], F32, name="shift")
                nc.vector.tensor_mul(out=shift[:], in0=minus_mean[:], in1=rstd[:])
                nc.scalar.activation(
                    out=normed[i][:], in_=x_sb[i][:], func=ACT.Identity, scale=rstd[:], bias=shift[:]
                )

        for i in range(TOKEN_TILES + 1):
            for c in range(CHUNKS):
                if i < TOKEN_TILES:
                    nc.vector.bn_stats(
                        out=stats[i][:, c, :], in_=x_sb[i][:, STATS_CHUNK * c : STATS_CHUNK * (c + 1)]
                    )
                if i > 0 and c == 0:
                    nc.vector.bn_aggr(out=mean_var[i - 1][:], in_=stats[i - 1][:].rearrange("p c s -> p (c s)"))
                if i > 0 and c == 1:
                    normalise(i - 1)

        for u in range(EARLY_SCALAR, EARLY_PIECES):
            regroup_piece(u, nc.vector.tensor_copy)
        for u in range(EARLY_SCALAR, EARLY_PIECES):
            quantise_piece(u)

        h_rows = keep.tile([P, D_SQUARES, TOKENS], BF16, name="h_rows")
        h_codes = keep.tile([P, PASSES, TOKENS], U32, name="h_codes", align_bytes=64)
        h_scales = keep.tile([P, PASSES, TOKENS], U8, name="h_scales", align_bytes=64)
        for g in range(PASSES):
            for j in range(PACK * g, PACK * (g + 1)):
                square = psum.tile([P, BANK], F32, tag="bank", name="square")
                for i in range(TOKEN_TILES):
                    nc.tensor.transpose(
                        square[:, P * i : P * (i + 1)], normed[i][:, P * j : P * (j + 1)], identity[:]
                    )
                nc.scalar.activation(
                    out=h_rows[:, j, :],
                    in_=square[:],
                    func=ACT.Identity,
                    scale=gain_cols[:, j : j + 1],
                    bias=gain_cols[:, D_SQUARES + j : D_SQUARES + j + 1],
                )
            h_grouped = regroup(lone, nc.vector.tensor_copy, h_rows[:, PACK * g : PACK * (g + 1), :])
            quantise_piece(g)
            quantise(h_grouped, h_codes[:, g, :], h_scales[:, g, :])

        block_sums = {}

        def multiply_piece(u):
            b, g = divmod(u, PASSES)
            width = piece_rows[u].shape[2]
            if g == 0:
                block_sums[b] = [
                    psum.tile([P, BANK], F32, tag="bank", name="sums%d" % i) for i in range(TOKEN_TILES)
                ]
            for i in range(TOKEN_TILES):
                nc.tensor.matmul_mx(
                    out=block_sums[b][i][:, :width],
                    lhsT=h_codes[:, g, P * i : P * (i + 1)].bitcast(FP8X4),
                    lhsT_scale=h_scales[:, g, P * i : P * (i + 1)],
                    rhs=block_codes[b][:, g, :width].bitcast(FP8X4),
                    rhs_scale=block_scales[b][:, g, :width],
                    start=(g == 0),
                    stop=(g == PASSES - 1),
                )

        def finish_block(b):
            width = piece_rows[PASSES * b].shape[2]
            for i in range(TOKEN_TILES):
                result = results.tile([P, BANK], F32, name="result")
                nc.vector.tensor_tensor(
                    out=result[:, :width],
                    in0=block_sums[b][i][:, :width],
                    in1=bias_all[:, BANK * b : BANK * b + width],
                    op=ALU.add,
                )
                if b < Q_BLOCKS:
                    nc.sync.dma_start(out=q_tiles[i][:, BANK * b : BANK * (b + 1)], in_=result[:])
                else:
                    nc.sync.dma_start(out=k_tiles[i], in_=result[:, 0:HEAD])
                    nc.sync.dma_start(out=v_tiles[i], in_=result[:, HEAD : 2 * HEAD])

        for u in range(EARLY_PIECES):
            multiply_piece(u)

        for b in range(2, BLOCKS):
            regroup_piece(PASSES * b + PASSES - 1, gpsimd_copy, lone)
            finish_block(b - 2)
            for g in range(PASSES - 1):
                regroup_piece(PASSES * b + g, nc.scalar.copy)
            for g in range(PASSES):
                quantise_piece(PASSES * b + g)
                multiply_piece(PASSES * b + g)
        finish_block(BLOCKS - 2)
        finish_block(BLOCKS - 1)
